import numpy as np
import ml_dtypes


def mxq(x, axis, fmt="e4m3"):
    dtype, down = {"e4m3": (ml_dtypes.float8_e4m3fn, 7), "e5m2": (ml_dtypes.float8_e5m2, 14)}[fmt]
    v = np.moveaxis(np.asarray(x, np.float32).astype(ml_dtypes.bfloat16).astype(np.float64), axis, -1)
    blocks = v.reshape(v.shape[:-1] + (-1, 32))
    amax = np.abs(blocks).max(-1, keepdims=True)
    byte = np.maximum(np.where(amax > 0, np.frexp(amax)[1] - 1 + 127, 0) - down, 1)
    scale = np.exp2(byte - 127.0)
    codes = (blocks / scale).astype(np.float32).astype(dtype).astype(np.float64)
    return np.moveaxis((codes * scale).reshape(v.shape), -1, axis)


WIDE = False


def mx_kscale(k):
    if not WIDE:
        return np.ones(k)
    levels = np.array([20, -20, 10, -10, 0])
    a = np.random.permutation(np.resize(levels, k // 512 * 4)).reshape(k // 512, 4)
    idx = np.arange(k)
    return np.exp2(a[idx // 512, idx % 128 // 32])


BF16 = ml_dtypes.bfloat16


def bf(x):
    return np.asarray(x, np.float32).astype(BF16)


def f64(x):
    return np.asarray(x).astype(np.float64)


B, N, V = 2, 32, 16
D = 128
E = 64
O = 512
K = D * E
T = B * N * V


def setup_inputs():
    sn = mx_kscale(T)[::V].reshape(B, N, 1)
    node = np.random.standard_normal((B, N, D)) * sn
    veh = np.random.standard_normal((B, V, E))
    W = np.random.standard_normal((O, K)) * 0.008
    b = np.random.standard_normal(O) * 0.3
    g = np.random.standard_normal((B, N, V, O)) * np.exp2(np.random.randint(-12, 1, (B, N, V, 1))) / sn[:, :, :, None]
    return {"node_embed": bf(node), "veh_fea": bf(veh), "W": bf(W), "b": bf(b), "grad_out": bf(g)}


def reference(node_embed, veh_fea, W, b, grad_out):
    node, veh = f64(node_embed), f64(veh_fea)
    z = node[:, :, None, :, None] * veh[:, None, :, None, :]
    t = node.shape[0] * node.shape[1] * veh.shape[1]
    z = z.reshape(t, node.shape[2] * veh.shape[2])
    g = f64(grad_out).reshape(t, -1)
    return mxq(g, 0, "e5m2").T @ mxq(z, 0, "e4m3")

@@ -1,0 +1,175 @@
+from contextlib import ExitStack
+
+import concourse.mybir as mybir
+
+BF16 = mybir.dt.bfloat16
+F32 = mybir.dt.float32
+U32 = mybir.dt.uint32
+U8 = mybir.dt.uint8
+E4M3X4 = mybir.dt.float8_e4m3fn_x4
+E5M2X4 = mybir.dt.float8_e5m2_x4
+
+P = 128
+PACK = 4
+B, N, V, D, E, O = 2, 32, 16, 128, 64, 512
+K = D * E
+T = B * N * V
+N_TILE = 512
+D_PER_TILE = N_TILE // E
+SLAB = E * PACK
+KT = K // N_TILE
+OT = O // P
+
+FLOPS = 2 * T * O * K
+BYTES = 4 * O * K + 2 * (T * O + B * N * D + B * V * E)
+
+PIN = False
+QG_AFTER = [2,4]
+STORE_GROUPS = [1,1,2,2,2,2,2,2,1,1]
+Z_BUFS = 4
+C_BUFS = 10
+S_BUFS = 3
+SCALAR_PERIOD = 1
+SCALAR_SLABS = ()
+TAIL_V = [1,3]
+
+
+def tile_bilinearpooling_kernel(tc, node_embed, veh_fea, W, b, grad_out, out):
+    nc = tc.nc
+    with ExitStack() as ctx:
+        if PIN:
+            ctx.enter_context(tc.manual_schedule())
+        keep = ctx.enter_context(tc.tile_pool(name="keep", bufs=1))
+        zpool = ctx.enter_context(tc.tile_pool(name="zpool", bufs=Z_BUFS))
+        cpool = ctx.enter_context(tc.tile_pool(name="cpool", bufs=C_BUFS))
+        spool = ctx.enter_context(tc.tile_pool(name="spool", bufs=S_BUFS))
+        psum = ctx.enter_context(tc.psum_pool(name="psum", bufs=8))
+
+        g_raw = keep.tile([P, B, PACK * O], BF16)
+        veh_raw = keep.tile([P, B, SLAB], BF16)
+        node_raw = keep.tile([P, B, D], BF16)
+
+        def load_g(queue, bi):
+            queue.dma_start(
+                out=g_raw[:, bi], in_=grad_out[bi].rearrange("n (q j) o -> (n q) (j o)", j=PACK)
+            )
+
+        load_g(nc.scalar, 0)
+        for q in range(PACK):
+            src = veh_fea[:, PACK * q : PACK * (q + 1), :].rearrange("b j e -> b (j e)")
+            nc.sync.dma_start(out=veh_raw[q:P:PACK], in_=src.unsqueeze(0).to_broadcast([N, B, SLAB]))
+        for q in range(PACK):
+            nc.sync.dma_start(out=node_raw[q:P:PACK], in_=node_embed.rearrange("b n d -> n b d"))
+        load_g(nc.sync, 1)
+
+        node_f = keep.tile([P, B, D], F32)
+        nc.scalar.copy(out=node_f[:], in_=node_raw[:])
+        veh_g = keep.tile([P, B, SLAB], BF16)
+        nc.vector.tensor_copy(
+            out=veh_g[:].rearrange("p b (e j) -> p b e j", j=PACK),
+            in_=veh_raw[:].rearrange("p b (j e) -> p b e j", j=PACK),
+        )
+
+        g_grp = keep.tile([P, B, PACK * O], BF16, align_bytes=64)
+        g_codes = keep.tile([P, B, O], U32, align_bytes=64)
+        g_scales = keep.tile([P, B, O], U8, align_bytes=64)
+        for bi in range(B):
+            nc.scalar.copy(
+                out=g_grp[:, bi].rearrange("p (o j) -> p o j", j=PACK),
+                in_=g_raw[:, bi].rearrange("p (j o) -> p o j", j=PACK),
+            )
+
+        def quantise_g(bi):
+            nc.vector.quantize_mx(
+                out=g_codes[:, bi].bitcast(E5M2X4), scales=g_scales[:, bi], in_=g_grp[:, bi]
+            )
+
+        z_bf = {}
+        z_codes = {}
+        z_scales = {}
+
+        def gen(i):
+            kt, bi = divmod(i, B)
+            zb = zpool.tile([P, PACK * N_TILE], BF16, align_bytes=64)
+            z_bf[i] = zb
+            for dd in range(D_PER_TILE):
+                dcol = kt * D_PER_TILE + dd
+                dst = zb[:, dd * SLAB : (dd + 1) * SLAB]
+                if (i % SCALAR_PERIOD, dd) in SCALAR_SLABS:
+                    nc.scalar.activation(
+                        out=dst,
+                        in_=veh_g[:, bi],
+                        func=mybir.ActivationFunctionType.Copy,
+                        scale=node_f[:, bi, dcol : dcol + 1],
+                    )
+                else:
+                    nc.vector.tensor_scalar_mul(
+                        out=dst, in0=veh_g[:, bi], scalar1=node_f[:, bi, dcol : dcol + 1]
+                    )
+
+        def quantise(i):
+            zc = cpool.tile([P, N_TILE], U32, align_bytes=64)
+            zs = cpool.tile([P, N_TILE], U8, align_bytes=64)
+            z_codes[i] = zc
+            z_scales[i] = zs
+            nc.vector.quantize_mx(out=zc[:].bitcast(E4M3X4), scales=zs[:], in_=z_bf[i][:])
+
+        group_of = {}
+        first = 0
+        for width in STORE_GROUPS:
+            for kt in range(first, first + width):
+                group_of[kt] = (first, width)
+            first += width
+        assert first == KT
+
+        acc = {}
+        stage = {}
+
+        def multiply(i):
+            kt, bi = divmod(i, B)
+            for ot in range(OT):
+                if bi == 0:
+                    acc[ot] = psum.tile([P, N_TILE], F32, name="acc%d" % ot, tag="acc")
+                cols = slice(ot * P, (ot + 1) * P)
+                nc.tensor.matmul_mx(
+                    out=acc[ot][:],
+                    lhsT=g_codes[:, bi, cols].bitcast(E5M2X4),
+                    lhsT_scale=g_scales[:, bi, cols],
+                    rhs=z_codes[i][:].bitcast(E4M3X4),
+                    rhs_scale=z_scales[i][:],
+                    start=(bi == 0),
+                    stop=(bi == B - 1),
+                )
+            if bi < B - 1:
+                return
+            first_kt, width = group_of[kt]
+            for ot in range(OT):
+                if kt == first_kt:
+                    stage[ot] = spool.tile(
+                        [P, width * N_TILE], F32, name="stage%d" % ot, tag="stage%d" % ot
+                    )
+                part = stage[ot][:, (kt - first_kt) * N_TILE : (kt - first_kt + 1) * N_TILE]
+                if kt == KT - 1 and ot in TAIL_V:
+                    nc.vector.tensor_copy(out=part, in_=acc[ot][:])
+                else:
+                    nc.scalar.copy(out=part, in_=acc[ot][:])
+                if kt == first_kt + width - 1:
+                    nc.sync.dma_start(
+                        out=out[ot * P : (ot + 1) * P, first_kt * N_TILE : (kt + 1) * N_TILE],
+                        in_=stage[ot][:],
+                    )
+
+        tiles = KT * B
+        g_done = 0
+        todo = 0
+        gen(0)
+        for i in range(tiles):
+            if i + 1 < tiles:
+                gen(i + 1)
+            quantise(i)
+            while g_done < B and i >= QG_AFTER[g_done]:
+                quantise_g(g_done)
+                g_done += 1
+            while todo <= i and todo % B < g_done:
+                multiply(todo)
+                todo += 1

@@ -23,7 +23,7 @@ OT = O // P
 FLOPS = 2 * T * O * K
 BYTES = 4 * O * K + 2 * (T * O + B * N * D + B * V * E)
 
-PIN = False
+PIN = True
 QG_AFTER = [2,4]
 STORE_GROUPS = [1,1,2,2,2,2,2,2,1,1]
 Z_BUFS = 4

@@ -19,26 +19,29 @@ D_PER_TILE = N_TILE // E
 SLAB = E * PACK
 KT = K // N_TILE
 OT = O // P
+TILES = KT * B
+G_PIECES = 2
+G_COLS = O // G_PIECES
 
 FLOPS = 2 * T * O * K
 BYTES = 4 * O * K + 2 * (T * O + B * N * D + B * V * E)
 
-PIN = True
-QG_AFTER = [2,4]
-STORE_GROUPS = [1,1,2,2,2,2,2,2,1,1]
-Z_BUFS = 4
+STORE_GROUPS = (1, 1, 2, 2, 2, 2, 2, 2, 1, 1)
+Z_BUFS = 6
 C_BUFS = 10
 S_BUFS = 3
-SCALAR_PERIOD = 1
-SCALAR_SLABS = ()
-TAIL_V = [1,3]
+SCALAR_LEAD = 3
+TAIL_V = (1, 3)
+
+
+def scalar_builds(i, dd):
+    return False
 
 
 def tile_bilinearpooling_kernel(tc, node_embed, veh_fea, W, b, grad_out, out):
     nc = tc.nc
     with ExitStack() as ctx:
-        if PIN:
-            ctx.enter_context(tc.manual_schedule())
+        ctx.enter_context(tc.manual_schedule())
         keep = ctx.enter_context(tc.tile_pool(name="keep", bufs=1))
         zpool = ctx.enter_context(tc.tile_pool(name="zpool", bufs=Z_BUFS))
         cpool = ctx.enter_context(tc.tile_pool(name="cpool", bufs=C_BUFS))
@@ -49,18 +52,14 @@ def tile_bilinearpooling_kernel(tc, node_embed, veh_fea, W, b, grad_out, out):
         veh_raw = keep.tile([P, B, SLAB], BF16)
         node_raw = keep.tile([P, B, D], BF16)
 
-        def load_g(queue, bi):
-            queue.dma_start(
+        for bi in range(B):
+            nc.gpsimd.dma_start(
                 out=g_raw[:, bi], in_=grad_out[bi].rearrange("n (q j) o -> (n q) (j o)", j=PACK)
             )
-
-        load_g(nc.scalar, 0)
         for q in range(PACK):
             src = veh_fea[:, PACK * q : PACK * (q + 1), :].rearrange("b j e -> b (j e)")
             nc.sync.dma_start(out=veh_raw[q:P:PACK], in_=src.unsqueeze(0).to_broadcast([N, B, SLAB]))
-        for q in range(PACK):
-            nc.sync.dma_start(out=node_raw[q:P:PACK], in_=node_embed.rearrange("b n d -> n b d"))
-        load_g(nc.sync, 1)
+            nc.scalar.dma_start(out=node_raw[q:P:PACK], in_=node_embed.rearrange("b n d -> n b d"))
 
         node_f = keep.tile([P, B, D], F32)
         nc.scalar.copy(out=node_f[:], in_=node_raw[:])
@@ -70,49 +69,45 @@ def tile_bilinearpooling_kernel(tc, node_embed, veh_fea, W, b, grad_out, out):
             in_=veh_raw[:].rearrange("p b (j e) -> p b e j", j=PACK),
         )
 
-        g_grp = keep.tile([P, B, PACK * O], BF16, align_bytes=64)
-        g_codes = keep.tile([P, B, O], U32, align_bytes=64)
-        g_scales = keep.tile([P, B, O], U8, align_bytes=64)
-        for bi in range(B):
-            nc.scalar.copy(
-                out=g_grp[:, bi].rearrange("p (o j) -> p o j", j=PACK),
-                in_=g_raw[:, bi].rearrange("p (j o) -> p o j", j=PACK),
-            )
-
-        def quantise_g(bi):
-            nc.vector.quantize_mx(
-                out=g_codes[:, bi].bitcast(E5M2X4), scales=g_scales[:, bi], in_=g_grp[:, bi]
-            )
-
         z_bf = {}
         z_codes = {}
         z_scales = {}
 
-        def gen(i):
+        def build(i, on_scalar):
+            if not 0 <= i < TILES:
+                return
             kt, bi = divmod(i, B)
-            zb = zpool.tile([P, PACK * N_TILE], BF16, align_bytes=64)
-            z_bf[i] = zb
             for dd in range(D_PER_TILE):
+                if scalar_builds(i, dd) != on_scalar:
+                    continue
+                if i not in z_bf:
+                    z_bf[i] = zpool.tile([P, PACK * N_TILE], BF16, name="zb", align_bytes=64)
                 dcol = kt * D_PER_TILE + dd
-                dst = zb[:, dd * SLAB : (dd + 1) * SLAB]
-                if (i % SCALAR_PERIOD, dd) in SCALAR_SLABS:
+                dst = z_bf[i][:, dd * SLAB : (dd + 1) * SLAB]
+                factor = node_f[:, bi, dcol : dcol + 1]
+                if on_scalar:
                     nc.scalar.activation(
-                        out=dst,
-                        in_=veh_g[:, bi],
-                        func=mybir.ActivationFunctionType.Copy,
-                        scale=node_f[:, bi, dcol : dcol + 1],
+                        out=dst, in_=veh_g[:, bi], func=mybir.ActivationFunctionType.Copy, scale=factor
                     )
                 else:
-                    nc.vector.tensor_scalar_mul(
-                        out=dst, in0=veh_g[:, bi], scalar1=node_f[:, bi, dcol : dcol + 1]
-                    )
+                    nc.vector.tensor_scalar_mul(out=dst, in0=veh_g[:, bi], scalar1=factor)
 
-        def quantise(i):
-            zc = cpool.tile([P, N_TILE], U32, align_bytes=64)
-            zs = cpool.tile([P, N_TILE], U8, align_bytes=64)
-            z_codes[i] = zc
-            z_scales[i] = zs
-            nc.vector.quantize_mx(out=zc[:].bitcast(E4M3X4), scales=zs[:], in_=z_bf[i][:])
+        for i in range(SCALAR_LEAD):
+            build(i, True)
+
+        g_grp = keep.tile([P, B, PACK * O], BF16, align_bytes=64)
+        g_codes = keep.tile([P, B, O], U32, align_bytes=64)
+        g_scales = keep.tile([P, B, O], U8, align_bytes=64)
+        for piece in range(B * G_PIECES):
+            bi, part = divmod(piece, G_PIECES)
+            nc.scalar.copy(
+                out=g_grp[:, bi, part * PACK * G_COLS : (part + 1) * PACK * G_COLS].rearrange(
+                    "p (o j) -> p o j", j=PACK
+                ),
+                in_=g_raw[:, bi].rearrange("p (j o) -> p o j", j=PACK)[
+                    :, part * G_COLS : (part + 1) * G_COLS, :
+                ],
+            )
 
         group_of = {}
         first = 0
@@ -124,52 +119,71 @@ def tile_bilinearpooling_kernel(tc, node_embed, veh_fea, W, b, grad_out, out):
 
         acc = {}
         stage = {}
+        written = {"g": 0, "z": 0, "pass": 0}
 
-        def multiply(i):
+        def one_pass(i, ot):
             kt, bi = divmod(i, B)
-            for ot in range(OT):
-                if bi == 0:
-                    acc[ot] = psum.tile([P, N_TILE], F32, name="acc%d" % ot, tag="acc")
-                cols = slice(ot * P, (ot + 1) * P)
-                nc.tensor.matmul_mx(
-                    out=acc[ot][:],
-                    lhsT=g_codes[:, bi, cols].bitcast(E5M2X4),
-                    lhsT_scale=g_scales[:, bi, cols],
-                    rhs=z_codes[i][:].bitcast(E4M3X4),
-                    rhs_scale=z_scales[i][:],
-                    start=(bi == 0),
-                    stop=(bi == B - 1),
-                )
+            if bi == 0:
+                acc[ot] = psum.tile([P, N_TILE], F32, name="acc%d" % ot, tag="acc")
+            cols = slice(ot * P, (ot + 1) * P)
+            nc.tensor.matmul_mx(
+                out=acc[ot][:],
+                lhsT=g_codes[:, bi, cols].bitcast(E5M2X4),
+                lhsT_scale=g_scales[:, bi, cols],
+                rhs=z_codes[i][:].bitcast(E4M3X4),
+                rhs_scale=z_scales[i][:],
+                start=(bi == 0),
+                stop=(bi == B - 1),
+            )
             if bi < B - 1:
                 return
             first_kt, width = group_of[kt]
-            for ot in range(OT):
-                if kt == first_kt:
-                    stage[ot] = spool.tile(
-                        [P, width * N_TILE], F32, name="stage%d" % ot, tag="stage%d" % ot
-                    )
-                part = stage[ot][:, (kt - first_kt) * N_TILE : (kt - first_kt + 1) * N_TILE]
-                if kt == KT - 1 and ot in TAIL_V:
-                    nc.vector.tensor_copy(out=part, in_=acc[ot][:])
-                else:
-                    nc.scalar.copy(out=part, in_=acc[ot][:])
-                if kt == first_kt + width - 1:
-                    nc.sync.dma_start(
-                        out=out[ot * P : (ot + 1) * P, first_kt * N_TILE : (kt + 1) * N_TILE],
-                        in_=stage[ot][:],
-                    )
+            if kt == first_kt:
+                stage[ot] = spool.tile([P, width * N_TILE], F32, name="stage%d" % ot, tag="stage%d" % ot)
+            part = stage[ot][:, (kt - first_kt) * N_TILE : (kt - first_kt + 1) * N_TILE]
+            if kt == KT - 1 and ot in TAIL_V:
+                nc.vector.tensor_copy(out=part, in_=acc[ot][:])
+            else:
+                nc.scalar.copy(out=part, in_=acc[ot][:])
+            if kt == first_kt + width - 1:
+                nc.sync.dma_start(
+                    out=out[ot * P : (ot + 1) * P, first_kt * N_TILE : (kt + 1) * N_TILE], in_=stage[ot][:]
+                )
 
-        tiles = KT * B
-        g_done = 0
-        todo = 0
-        gen(0)
-        for i in range(tiles):
-            if i + 1 < tiles:
-                gen(i + 1)
+        def passes():
+            while written["pass"] < TILES * OT:
+                i, ot = divmod(written["pass"], OT)
+                if i >= written["z"] or (i % B) * G_PIECES + ot * G_PIECES // OT >= written["g"]:
+                    return
+                one_pass(i, ot)
+                written["pass"] += 1
+
+        def quantise_g(piece):
+            if not 0 <= piece < B * G_PIECES:
+                return
+            bi, part = divmod(piece, G_PIECES)
+            cols = slice(part * G_COLS, (part + 1) * G_COLS)
+            nc.vector.quantize_mx(
+                out=g_codes[:, bi, cols].bitcast(E5M2X4),
+                scales=g_scales[:, bi, cols],
+                in_=g_grp[:, bi, part * PACK * G_COLS : (part + 1) * PACK * G_COLS],
+            )
+            written["g"] = piece + 1
+            passes()
+
+        def quantise(i):
+            zc = cpool.tile([P, N_TILE], U32, align_bytes=64)
+            zs = cpool.tile([P, N_TILE], U8, align_bytes=64)
+            z_codes[i] = zc
+            z_scales[i] = zs
+            nc.vector.quantize_mx(out=zc[:].bitcast(E4M3X4), scales=zs[:], in_=z_bf[i][:])
+            written["z"] = i + 1
+            passes()
+
+        build(0, False)
+        for i in range(TILES):
+            build(i + SCALAR_LEAD, True)
+            build(i + 1, False)
+            quantise_g(2 * i - 1)
             quantise(i)
-            while g_done < B and i >= QG_AFTER[g_done]:
-                quantise_g(g_done)
-                g_done += 1
-            while todo <= i and todo % B < g_done:
-                multiply(todo)
-                todo += 1
+            quantise_g(2 * i)

@@ -35,7 +35,7 @@ TAIL_V = (1, 3)
 
 
 def scalar_builds(i, dd):
-    return False
+    return i % 2 == 1 and dd == D_PER_TILE - 1
 
 
 def tile_bilinearpooling_kernel(tc, node_embed, veh_fea, W, b, grad_out, out):

@@ -1,6 +1,7 @@
 from contextlib import ExitStack
 
 import concourse.mybir as mybir
+from concourse.masks import make_identity
 
 BF16 = mybir.dt.bfloat16
 F32 = mybir.dt.float32
@@ -11,31 +12,29 @@ E5M2X4 = mybir.dt.float8_e5m2_x4
 
 P = 128
 PACK = 4
+PASSES = 2
 B, N, V, D, E, O = 2, 32, 16, 128, 64, 512
 K = D * E
 T = B * N * V
+V_PER_PART = PASSES * PACK
 N_TILE = 512
 D_PER_TILE = N_TILE // E
 SLAB = E * PACK
 KT = K // N_TILE
 OT = O // P
-TILES = KT * B
-G_PIECES = 2
-G_COLS = O // G_PIECES
+G_COLS = 256
+G_HALVES = O // G_COLS
 
 FLOPS = 2 * T * O * K
 BYTES = 4 * O * K + 2 * (T * O + B * N * D + B * V * E)
 
 STORE_GROUPS = (1, 1, 2, 2, 2, 2, 2, 2, 1, 1)
-Z_BUFS = 6
-C_BUFS = 10
+Z_BUFS = 3
+C_BUFS = 4
 S_BUFS = 3
-SCALAR_LEAD = 3
 TAIL_V = (1, 3)
-
-
-def scalar_builds(i, dd):
-    return i % 2 == 1 and dd == D_PER_TILE - 1
+G_BEFORE = {0: (0,), 1: (3,)}
+G_AFTER = {0: (1, 2)}
 
 
 def tile_bilinearpooling_kernel(tc, node_embed, veh_fea, W, b, grad_out, out):
@@ -48,66 +47,81 @@ def tile_bilinearpooling_kernel(tc, node_embed, veh_fea, W, b, grad_out, out):
         spool = ctx.enter_context(tc.tile_pool(name="spool", bufs=S_BUFS))
         psum = ctx.enter_context(tc.psum_pool(name="psum", bufs=8))
 
-        g_raw = keep.tile([P, B, PACK * O], BF16)
-        veh_raw = keep.tile([P, B, SLAB], BF16)
-        node_raw = keep.tile([P, B, D], BF16)
-
-        for bi in range(B):
-            nc.gpsimd.dma_start(
-                out=g_raw[:, bi], in_=grad_out[bi].rearrange("n (q j) o -> (n q) (j o)", j=PACK)
+        node_nat = keep.tile([P, 2 * D], BF16)
+        veh_raw = keep.tile([P, PASSES, SLAB], BF16)
+        g_nat = keep.tile([P, PASSES, PACK, O], BF16)
+        queues = (nc.sync, nc.scalar)
+        g_rows = grad_out.rearrange("b n (h c j) o -> (b n h) c (j o)", c=PASSES, j=PACK)
+        for half in range(2):
+            queues[half].dma_start(
+                out=node_nat[half:P:2, 0:D], in_=node_embed.rearrange("b n d -> (b n) d")
             )
-        for q in range(PACK):
-            src = veh_fea[:, PACK * q : PACK * (q + 1), :].rearrange("b j e -> b (j e)")
-            nc.sync.dma_start(out=veh_raw[q:P:PACK], in_=src.unsqueeze(0).to_broadcast([N, B, SLAB]))
-            nc.scalar.dma_start(out=node_raw[q:P:PACK], in_=node_embed.rearrange("b n d -> n b d"))
+        for bi in range(B):
+            for half in range(2):
+                src = veh_fea[bi, V_PER_PART * half : V_PER_PART * (half + 1), :]
+                queues[bi].dma_start(
+                    out=veh_raw[bi * (P // B) + half : (bi + 1) * (P // B) : 2].rearrange("p c f -> p (c f)"),
+                    in_=src.rearrange("w e -> (w e)").unsqueeze(0).to_broadcast([N, PASSES * SLAB]),
+                )
+        for c in range(PASSES):
+            queues[c].dma_start(out=g_nat[:, c].rearrange("p j o -> p (j o)"), in_=g_rows[:, c])
 
-        node_f = keep.tile([P, B, D], F32)
-        nc.scalar.copy(out=node_f[:], in_=node_raw[:])
-        veh_g = keep.tile([P, B, SLAB], BF16)
+        ident = keep.tile([P, P], BF16)
+        make_identity(nc, ident[:])
+        nc.vector.memset(node_nat[:, D : 2 * D], 0.0)
+        perm = keep.tile([P, P], BF16)
         nc.vector.tensor_copy(
-            out=veh_g[:].rearrange("p b (e j) -> p b e j", j=PACK),
-            in_=veh_raw[:].rearrange("p b (j e) -> p b e j", j=PACK),
+            out=perm[:].rearrange("u (a k h r) -> u a k h r", a=4, k=4, h=2, r=4),
+            in_=ident[:].rearrange("u (a h k r) -> u a k h r", a=4, h=2, k=4, r=4),
         )
+
+        node_ps = psum.tile([P, 2 * D], F32, tag="acc")
+        nc.tensor.matmul(out=node_ps[:], lhsT=perm[:], rhs=node_nat[:], start=True, stop=True)
+        node_f = keep.tile([P, D], F32)
+        nc.scalar.copy(out=node_f[:], in_=node_ps[:, 0:D])
+        veh_g = keep.tile([P, PASSES, SLAB], BF16)
+        nc.vector.tensor_copy(
+            out=veh_g[:].rearrange("p c (e j) -> p c e j", j=PACK),
+            in_=veh_raw[:].rearrange("p c (j e) -> p c e j", j=PACK),
+        )
+
+        g_grp = keep.tile([P, PASSES, PACK * O], BF16, align_bytes=64)
+        g_codes = keep.tile([P, PASSES, O], U32, align_bytes=64)
+        g_scales = keep.tile([P, PASSES, O], U8, align_bytes=64)
+        for piece in range(G_HALVES * PASSES):
+            oh, c = divmod(piece, PASSES)
+            g_ps = psum.tile([P, PACK, G_COLS], BF16, tag="acc")
+            for j in range(PACK):
+                nc.tensor.matmul(
+                    out=g_ps[:, j, :],
+                    lhsT=perm[:],
+                    rhs=g_nat[:, c, j, oh * G_COLS : (oh + 1) * G_COLS],
+                    start=True,
+                    stop=True,
+                )
+            nc.scalar.copy(
+                out=g_grp[:, c, oh * PACK * G_COLS : (oh + 1) * PACK * G_COLS].rearrange(
+                    "p (o j) -> p o j", j=PACK
+                ),
+                in_=g_ps[:].rearrange("p j o -> p o j"),
+            )
 
         z_bf = {}
         z_codes = {}
         z_scales = {}
 
-        def build(i, on_scalar):
-            if not 0 <= i < TILES:
+        def build(kt):
+            if kt >= KT:
                 return
-            kt, bi = divmod(i, B)
+            zb = zpool.tile([P, PASSES, PACK * N_TILE], BF16, align_bytes=64)
+            z_bf[kt] = zb
             for dd in range(D_PER_TILE):
-                if scalar_builds(i, dd) != on_scalar:
-                    continue
-                if i not in z_bf:
-                    z_bf[i] = zpool.tile([P, PACK * N_TILE], BF16, name="zb", align_bytes=64)
                 dcol = kt * D_PER_TILE + dd
-                dst = z_bf[i][:, dd * SLAB : (dd + 1) * SLAB]
-                factor = node_f[:, bi, dcol : dcol + 1]
-                if on_scalar:
-                    nc.scalar.activation(
-                        out=dst, in_=veh_g[:, bi], func=mybir.ActivationFunctionType.Copy, scale=factor
-                    )
-                else:
-                    nc.vector.tensor_scalar_mul(out=dst, in0=veh_g[:, bi], scalar1=factor)
-
-        for i in range(SCALAR_LEAD):
-            build(i, True)
-
-        g_grp = keep.tile([P, B, PACK * O], BF16, align_bytes=64)
-        g_codes = keep.tile([P, B, O], U32, align_bytes=64)
-        g_scales = keep.tile([P, B, O], U8, align_bytes=64)
-        for piece in range(B * G_PIECES):
-            bi, part = divmod(piece, G_PIECES)
-            nc.scalar.copy(
-                out=g_grp[:, bi, part * PACK * G_COLS : (part + 1) * PACK * G_COLS].rearrange(
-                    "p (o j) -> p o j", j=PACK
-                ),
-                in_=g_raw[:, bi].rearrange("p (j o) -> p o j", j=PACK)[
-                    :, part * G_COLS : (part + 1) * G_COLS, :
-                ],
-            )
+                nc.vector.tensor_scalar_mul(
+                    out=zb[:, :, dd * SLAB : (dd + 1) * SLAB],
+                    in0=veh_g[:],
+                    scalar1=node_f[:, dcol : dcol + 1],
+                )
 
         group_of = {}
         first = 0
@@ -121,21 +135,21 @@ def tile_bilinearpooling_kernel(tc, node_embed, veh_fea, W, b, grad_out, out):
         stage = {}
         written = {"g": 0, "z": 0, "pass": 0}
 
-        def one_pass(i, ot):
-            kt, bi = divmod(i, B)
-            if bi == 0:
+        def one_pass(kt, ot, c):
+            if c == 0:
                 acc[ot] = psum.tile([P, N_TILE], F32, name="acc%d" % ot, tag="acc")
-            cols = slice(ot * P, (ot + 1) * P)
+            rows = slice(ot * P, (ot + 1) * P)
+            cols = slice(c * N_TILE, (c + 1) * N_TILE)
             nc.tensor.matmul_mx(
                 out=acc[ot][:],
-                lhsT=g_codes[:, bi, cols].bitcast(E5M2X4),
-                lhsT_scale=g_scales[:, bi, cols],
-                rhs=z_codes[i][:].bitcast(E4M3X4),
-                rhs_scale=z_scales[i][:],
-                start=(bi == 0),
-                stop=(bi == B - 1),
+                lhsT=g_codes[:, c, rows].bitcast(E5M2X4),
+                lhsT_scale=g_scales[:, c, rows],
+                rhs=z_codes[kt][:, cols].bitcast(E4M3X4),
+                rhs_scale=z_scales[kt][:, cols],
+                start=(c == 0),
+                stop=(c == PASSES - 1),
             )
-            if bi < B - 1:
+            if c < PASSES - 1:
                 return
             first_kt, width = group_of[kt]
             if kt == first_kt:
@@ -151,39 +165,41 @@ def tile_bilinearpooling_kernel(tc, node_embed, veh_fea, W, b, grad_out, out):
                 )
 
         def passes():
-            while written["pass"] < TILES * OT:
-                i, ot = divmod(written["pass"], OT)
-                if i >= written["z"] or (i % B) * G_PIECES + ot * G_PIECES // OT >= written["g"]:
+            while written["pass"] < KT * OT * PASSES:
+                kt, rest = divmod(written["pass"], OT * PASSES)
+                ot, c = divmod(rest, PASSES)
+                if kt >= written["z"] or (ot * P // G_COLS) * PASSES + c >= written["g"]:
                     return
-                one_pass(i, ot)
+                one_pass(kt, ot, c)
                 written["pass"] += 1
 
         def quantise_g(piece):
-            if not 0 <= piece < B * G_PIECES:
-                return
-            bi, part = divmod(piece, G_PIECES)
-            cols = slice(part * G_COLS, (part + 1) * G_COLS)
+            oh, c = divmod(piece, PASSES)
+            cols = slice(oh * G_COLS, (oh + 1) * G_COLS)
             nc.vector.quantize_mx(
-                out=g_codes[:, bi, cols].bitcast(E5M2X4),
-                scales=g_scales[:, bi, cols],
-                in_=g_grp[:, bi, part * PACK * G_COLS : (part + 1) * PACK * G_COLS],
+                out=g_codes[:, c, cols].bitcast(E5M2X4),
+                scales=g_scales[:, c, cols],
+                in_=g_grp[:, c, oh * PACK * G_COLS : (oh + 1) * PACK * G_COLS],
             )
             written["g"] = piece + 1
             passes()
 
-        def quantise(i):
-            zc = cpool.tile([P, N_TILE], U32, align_bytes=64)
-            zs = cpool.tile([P, N_TILE], U8, align_bytes=64)
-            z_codes[i] = zc
-            z_scales[i] = zs
-            nc.vector.quantize_mx(out=zc[:].bitcast(E4M3X4), scales=zs[:], in_=z_bf[i][:])
-            written["z"] = i + 1
+        def quantise(kt):
+            zc = cpool.tile([P, PASSES * N_TILE], U32, align_bytes=64)
+            zs = cpool.tile([P, PASSES * N_TILE], U8, align_bytes=64)
+            z_codes[kt] = zc
+            z_scales[kt] = zs
+            nc.vector.quantize_mx(
+                out=zc[:].bitcast(E4M3X4), scales=zs[:], in_=z_bf[kt][:].rearrange("p c f -> p (c f)")
+            )
+            written["z"] = kt + 1
             passes()
 
-        build(0, False)
-        for i in range(TILES):
-            build(i + SCALAR_LEAD, True)
-            build(i + 1, False)
-            quantise_g(2 * i - 1)
-            quantise(i)
-            quantise_g(2 * i)
+        build(0)
+        for kt in range(KT):
+            build(kt + 1)
+            for piece in G_BEFORE.get(kt, ()):
+                quantise_g(piece)
+            quantise(kt)
+            for piece in G_AFTER.get(kt, ()):
+                quantise_g(piece)

@@ -33,8 +33,11 @@ Z_BUFS = 3
 C_BUFS = 4
 S_BUFS = 3
 TAIL_V = (1, 3)
-G_BEFORE = {0: (0,), 1: (3,)}
-G_AFTER = {0: (1, 2)}
+G_BEFORE = {1: (2, 3)}
+G_AFTER = {0: (0, 1)}
+LEAD = 2
+CODE_PAD = 48
+PLANE_SLOT = 256
 
 
 def tile_bilinearpooling_kernel(tc, node_embed, veh_fea, W, b, grad_out, out):
@@ -86,8 +89,9 @@ def tile_bilinearpooling_kernel(tc, node_embed, veh_fea, W, b, grad_out, out):
         )
 
         g_grp = keep.tile([P, PASSES, PACK * O], BF16, align_bytes=64)
-        g_codes = keep.tile([P, PASSES, O], U32, align_bytes=64)
-        g_scales = keep.tile([P, PASSES, O], U8, align_bytes=64)
+        g_words = keep.tile([P, CODE_PAD + PASSES * O], U32, align_bytes=256)
+        g_codes = g_words[:, CODE_PAD:].rearrange("p (c o) -> p c o", c=PASSES)
+        g_scales = keep.tile([P, PASSES, OT, PLANE_SLOT], U8, align_bytes=256)
         for piece in range(G_HALVES * PASSES):
             oh, c = divmod(piece, PASSES)
             g_ps = psum.tile([P, PACK, G_COLS], BF16, tag="acc")
@@ -110,12 +114,13 @@ def tile_bilinearpooling_kernel(tc, node_embed, veh_fea, W, b, grad_out, out):
         z_codes = {}
         z_scales = {}
 
-        def build(kt):
+        def build(kt, lo, hi):
             if kt >= KT:
                 return
-            zb = zpool.tile([P, PASSES, PACK * N_TILE], BF16, align_bytes=64)
-            z_bf[kt] = zb
-            for dd in range(D_PER_TILE):
+            if lo == 0:
+                z_bf[kt] = zpool.tile([P, PASSES, PACK * N_TILE], BF16, name="zb", align_bytes=64)
+            zb = z_bf[kt]
+            for dd in range(lo, hi):
                 dcol = kt * D_PER_TILE + dd
                 nc.vector.tensor_scalar_mul(
                     out=zb[:, :, dd * SLAB : (dd + 1) * SLAB],
@@ -143,7 +148,7 @@ def tile_bilinearpooling_kernel(tc, node_embed, veh_fea, W, b, grad_out, out):
             nc.tensor.matmul_mx(
                 out=acc[ot][:],
                 lhsT=g_codes[:, c, rows].bitcast(E5M2X4),
-                lhsT_scale=g_scales[:, c, rows],
+                lhsT_scale=g_scales[:, c, ot, 0:P],
                 rhs=z_codes[kt][:, cols].bitcast(E4M3X4),
                 rhs_scale=z_scales[kt][:, cols],
                 start=(c == 0),
@@ -175,18 +180,18 @@ def tile_bilinearpooling_kernel(tc, node_embed, veh_fea, W, b, grad_out, out):
 
         def quantise_g(piece):
             oh, c = divmod(piece, PASSES)
-            cols = slice(oh * G_COLS, (oh + 1) * G_COLS)
-            nc.vector.quantize_mx(
-                out=g_codes[:, c, cols].bitcast(E5M2X4),
-                scales=g_scales[:, c, cols],
-                in_=g_grp[:, c, oh * PACK * G_COLS : (oh + 1) * PACK * G_COLS],
-            )
+            for ot in range(oh * G_COLS // P, (oh + 1) * G_COLS // P):
+                nc.vector.quantize_mx(
+                    out=g_codes[:, c, ot * P : (ot + 1) * P].bitcast(E5M2X4),
+                    scales=g_scales[:, c, ot, 0:P],
+                    in_=g_grp[:, c, ot * PACK * P : (ot + 1) * PACK * P],
+                )
             written["g"] = piece + 1
             passes()
 
         def quantise(kt):
-            zc = cpool.tile([P, PASSES * N_TILE], U32, align_bytes=64)
-            zs = cpool.tile([P, PASSES * N_TILE], U8, align_bytes=64)
+            zc = cpool.tile([P, PASSES * N_TILE], U32, align_bytes=256)
+            zs = cpool.tile([P, PASSES * N_TILE], U8, align_bytes=256)
             z_codes[kt] = zc
             z_scales[kt] = zs
             nc.vector.quantize_mx(
@@ -195,11 +200,12 @@ def tile_bilinearpooling_kernel(tc, node_embed, veh_fea, W, b, grad_out, out):
             written["z"] = kt + 1
             passes()
 
-        build(0)
+        build(0, 0, D_PER_TILE)
         for kt in range(KT):
-            build(kt + 1)
+            build(kt + 1, 0, LEAD)
             for piece in G_BEFORE.get(kt, ()):
                 quantise_g(piece)
             quantise(kt)
             for piece in G_AFTER.get(kt, ()):
                 quantise_g(piece)
+            build(kt + 1, LEAD, D_PER_TILE)

@@ -1,7 +1,6 @@
 from contextlib import ExitStack
 
 import concourse.mybir as mybir
-from concourse.masks import make_identity
 
 BF16 = mybir.dt.bfloat16
 F32 = mybir.dt.float32
@@ -12,32 +11,31 @@ E5M2X4 = mybir.dt.float8_e5m2_x4
 
 P = 128
 PACK = 4
-PASSES = 2
 B, N, V, D, E, O = 2, 32, 16, 128, 64, 512
 K = D * E
 T = B * N * V
-V_PER_PART = PASSES * PACK
 N_TILE = 512
 D_PER_TILE = N_TILE // E
 SLAB = E * PACK
 KT = K // N_TILE
 OT = O // P
-G_COLS = 256
-G_HALVES = O // G_COLS
+TILES = KT * B
+G_PIECES = 2
+G_COLS = O // G_PIECES
 
 FLOPS = 2 * T * O * K
 BYTES = 4 * O * K + 2 * (T * O + B * N * D + B * V * E)
 
-STORE_GROUPS = (1, 1, 2, 2, 2, 2, 2, 2, 1, 1)
-Z_BUFS = 3
-C_BUFS = 4
+STORE_GROUPS = (1, 1, 2, 4, 4, 2, 1, 1)
+Z_BUFS = 6
+C_BUFS = 10
 S_BUFS = 3
+SCALAR_LEAD = 3
 TAIL_V = (1, 3)
-G_BEFORE = {1: (2, 3)}
-G_AFTER = {0: (0, 1)}
-LEAD = 2
-CODE_PAD = 48
-PLANE_SLOT = 256
+
+
+def scalar_builds(i, dd):
+    return i % 2 == 1 and dd == D_PER_TILE - 1
 
 
 def tile_bilinearpooling_kernel(tc, node_embed, veh_fea, W, b, grad_out, out):
@@ -50,83 +48,66 @@ def tile_bilinearpooling_kernel(tc, node_embed, veh_fea, W, b, grad_out, out):
         spool = ctx.enter_context(tc.tile_pool(name="spool", bufs=S_BUFS))
         psum = ctx.enter_context(tc.psum_pool(name="psum", bufs=8))
 
-        node_nat = keep.tile([P, 2 * D], BF16)
-        veh_raw = keep.tile([P, PASSES, SLAB], BF16)
-        g_nat = keep.tile([P, PASSES, PACK, O], BF16)
-        queues = (nc.sync, nc.scalar)
-        g_rows = grad_out.rearrange("b n (h c j) o -> (b n h) c (j o)", c=PASSES, j=PACK)
-        for half in range(2):
-            queues[half].dma_start(
-                out=node_nat[half:P:2, 0:D], in_=node_embed.rearrange("b n d -> (b n) d")
-            )
+        g_raw = keep.tile([P, B, PACK * O], BF16)
+        veh_raw = keep.tile([P, B, SLAB], BF16)
+        node_raw = keep.tile([P, B, D], BF16)
+
         for bi in range(B):
-            for half in range(2):
-                src = veh_fea[bi, V_PER_PART * half : V_PER_PART * (half + 1), :]
-                queues[bi].dma_start(
-                    out=veh_raw[bi * (P // B) + half : (bi + 1) * (P // B) : 2].rearrange("p c f -> p (c f)"),
-                    in_=src.rearrange("w e -> (w e)").unsqueeze(0).to_broadcast([N, PASSES * SLAB]),
-                )
-        for c in range(PASSES):
-            queues[c].dma_start(out=g_nat[:, c].rearrange("p j o -> p (j o)"), in_=g_rows[:, c])
-
-        ident = keep.tile([P, P], BF16)
-        make_identity(nc, ident[:])
-        nc.vector.memset(node_nat[:, D : 2 * D], 0.0)
-        perm = keep.tile([P, P], BF16)
-        nc.vector.tensor_copy(
-            out=perm[:].rearrange("u (a k h r) -> u a k h r", a=4, k=4, h=2, r=4),
-            in_=ident[:].rearrange("u (a h k r) -> u a k h r", a=4, h=2, k=4, r=4),
-        )
-
-        node_ps = psum.tile([P, 2 * D], F32, tag="acc")
-        nc.tensor.matmul(out=node_ps[:], lhsT=perm[:], rhs=node_nat[:], start=True, stop=True)
-        node_f = keep.tile([P, D], F32)
-        nc.scalar.copy(out=node_f[:], in_=node_ps[:, 0:D])
-        veh_g = keep.tile([P, PASSES, SLAB], BF16)
-        nc.vector.tensor_copy(
-            out=veh_g[:].rearrange("p c (e j) -> p c e j", j=PACK),
-            in_=veh_raw[:].rearrange("p c (j e) -> p c e j", j=PACK),
-        )
-
-        g_grp = keep.tile([P, PASSES, PACK * O], BF16, align_bytes=64)
-        g_words = keep.tile([P, CODE_PAD + PASSES * O], U32, align_bytes=256)
-        g_codes = g_words[:, CODE_PAD:].rearrange("p (c o) -> p c o", c=PASSES)
-        g_scales = keep.tile([P, PASSES, OT, PLANE_SLOT], U8, align_bytes=256)
-        for piece in range(G_HALVES * PASSES):
-            oh, c = divmod(piece, PASSES)
-            g_ps = psum.tile([P, PACK, G_COLS], BF16, tag="acc")
-            for j in range(PACK):
-                nc.tensor.matmul(
-                    out=g_ps[:, j, :],
-                    lhsT=perm[:],
-                    rhs=g_nat[:, c, j, oh * G_COLS : (oh + 1) * G_COLS],
-                    start=True,
-                    stop=True,
-                )
-            nc.scalar.copy(
-                out=g_grp[:, c, oh * PACK * G_COLS : (oh + 1) * PACK * G_COLS].rearrange(
-                    "p (o j) -> p o j", j=PACK
-                ),
-                in_=g_ps[:].rearrange("p j o -> p o j"),
+            nc.gpsimd.dma_start(
+                out=g_raw[:, bi], in_=grad_out[bi].rearrange("n (q j) o -> (n q) (j o)", j=PACK)
             )
+        for q in range(PACK):
+            src = veh_fea[:, PACK * q : PACK * (q + 1), :].rearrange("b j e -> b (j e)")
+            nc.sync.dma_start(out=veh_raw[q:P:PACK], in_=src.unsqueeze(0).to_broadcast([N, B, SLAB]))
+            nc.scalar.dma_start(out=node_raw[q:P:PACK], in_=node_embed.rearrange("b n d -> n b d"))
+
+        node_f = keep.tile([P, B, D], F32)
+        nc.scalar.copy(out=node_f[:], in_=node_raw[:])
+        veh_g = keep.tile([P, B, SLAB], BF16)
+        nc.vector.tensor_copy(
+            out=veh_g[:].rearrange("p b (e j) -> p b e j", j=PACK),
+            in_=veh_raw[:].rearrange("p b (j e) -> p b e j", j=PACK),
+        )
 
         z_bf = {}
         z_codes = {}
         z_scales = {}
 
-        def build(kt, lo, hi):
-            if kt >= KT:
+        def build(i, on_scalar):
+            if not 0 <= i < TILES:
                 return
-            if lo == 0:
-                z_bf[kt] = zpool.tile([P, PASSES, PACK * N_TILE], BF16, name="zb", align_bytes=64)
-            zb = z_bf[kt]
-            for dd in range(lo, hi):
+            kt, bi = divmod(i, B)
+            for dd in range(D_PER_TILE):
+                if scalar_builds(i, dd) != on_scalar:
+                    continue
+                if i not in z_bf:
+                    z_bf[i] = zpool.tile([P, PACK * N_TILE], BF16, name="zb", align_bytes=64)
                 dcol = kt * D_PER_TILE + dd
-                nc.vector.tensor_scalar_mul(
-                    out=zb[:, :, dd * SLAB : (dd + 1) * SLAB],
-                    in0=veh_g[:],
-                    scalar1=node_f[:, dcol : dcol + 1],
-                )
+                dst = z_bf[i][:, dd * SLAB : (dd + 1) * SLAB]
+                factor = node_f[:, bi, dcol : dcol + 1]
+                if on_scalar:
+                    nc.scalar.activation(
+                        out=dst, in_=veh_g[:, bi], func=mybir.ActivationFunctionType.Copy, scale=factor
+                    )
+                else:
+                    nc.vector.tensor_scalar_mul(out=dst, in0=veh_g[:, bi], scalar1=factor)
+
+        for i in range(SCALAR_LEAD):
+            build(i, True)
+
+        g_grp = keep.tile([P, B, PACK * O], BF16, align_bytes=64)
+        g_codes = keep.tile([P, B, O], U32, align_bytes=64)
+        g_scales = keep.tile([P, B, O], U8, align_bytes=64)
+        for piece in range(B * G_PIECES):
+            bi, part = divmod(piece, G_PIECES)
+            nc.scalar.copy(
+                out=g_grp[:, bi, part * PACK * G_COLS : (part + 1) * PACK * G_COLS].rearrange(
+                    "p (o j) -> p o j", j=PACK
+                ),
+                in_=g_raw[:, bi].rearrange("p (j o) -> p o j", j=PACK)[
+                    :, part * G_COLS : (part + 1) * G_COLS, :
+                ],
+            )
 
         group_of = {}
         first = 0
@@ -140,21 +121,21 @@ def tile_bilinearpooling_kernel(tc, node_embed, veh_fea, W, b, grad_out, out):
         stage = {}
         written = {"g": 0, "z": 0, "pass": 0}
 
-        def one_pass(kt, ot, c):
-            if c == 0:
+        def one_pass(i, ot):
+            kt, bi = divmod(i, B)
+            if bi == 0:
                 acc[ot] = psum.tile([P, N_TILE], F32, name="acc%d" % ot, tag="acc")
-            rows = slice(ot * P, (ot + 1) * P)
-            cols = slice(c * N_TILE, (c + 1) * N_TILE)
+            cols = slice(ot * P, (ot + 1) * P)
             nc.tensor.matmul_mx(
                 out=acc[ot][:],
-                lhsT=g_codes[:, c, rows].bitcast(E5M2X4),
-                lhsT_scale=g_scales[:, c, ot, 0:P],
-                rhs=z_codes[kt][:, cols].bitcast(E4M3X4),
-                rhs_scale=z_scales[kt][:, cols],
-                start=(c == 0),
-                stop=(c == PASSES - 1),
+                lhsT=g_codes[:, bi, cols].bitcast(E5M2X4),
+                lhsT_scale=g_scales[:, bi, cols],
+                rhs=z_codes[i][:].bitcast(E4M3X4),
+                rhs_scale=z_scales[i][:],
+                start=(bi == 0),
+                stop=(bi == B - 1),
             )
-            if c < PASSES - 1:
+            if bi < B - 1:
                 return
             first_kt, width = group_of[kt]
             if kt == first_kt:
@@ -170,42 +151,39 @@ def tile_bilinearpooling_kernel(tc, node_embed, veh_fea, W, b, grad_out, out):
                 )
 
         def passes():
-            while written["pass"] < KT * OT * PASSES:
-                kt, rest = divmod(written["pass"], OT * PASSES)
-                ot, c = divmod(rest, PASSES)
-                if kt >= written["z"] or (ot * P // G_COLS) * PASSES + c >= written["g"]:
+            while written["pass"] < TILES * OT:
+                i, ot = divmod(written["pass"], OT)
+                if i >= written["z"] or (i % B) * G_PIECES + ot * G_PIECES // OT >= written["g"]:
                     return
-                one_pass(kt, ot, c)
+                one_pass(i, ot)
                 written["pass"] += 1
 
         def quantise_g(piece):
-            oh, c = divmod(piece, PASSES)
-            for ot in range(oh * G_COLS // P, (oh + 1) * G_COLS // P):
-                nc.vector.quantize_mx(
-                    out=g_codes[:, c, ot * P : (ot + 1) * P].bitcast(E5M2X4),
-                    scales=g_scales[:, c, ot, 0:P],
-                    in_=g_grp[:, c, ot * PACK * P : (ot + 1) * PACK * P],
-                )
+            if not 0 <= piece < B * G_PIECES:
+                return
+            bi, part = divmod(piece, G_PIECES)
+            cols = slice(part * G_COLS, (part + 1) * G_COLS)
+            nc.vector.quantize_mx(
+                out=g_codes[:, bi, cols].bitcast(E5M2X4),
+                scales=g_scales[:, bi, cols],
+                in_=g_grp[:, bi, part * PACK * G_COLS : (part + 1) * PACK * G_COLS],
+            )
             written["g"] = piece + 1
             passes()
 
-        def quantise(kt):
-            zc = cpool.tile([P, PASSES * N_TILE], U32, align_bytes=256)
-            zs = cpool.tile([P, PASSES * N_TILE], U8, align_bytes=256)
-            z_codes[kt] = zc
-            z_scales[kt] = zs
-            nc.vector.quantize_mx(
-                out=zc[:].bitcast(E4M3X4), scales=zs[:], in_=z_bf[kt][:].rearrange("p c f -> p (c f)")
-            )
-            written["z"] = kt + 1
+        def quantise(i):
+            zc = cpool.tile([P, N_TILE], U32, align_bytes=64)
+            zs = cpool.tile([P, N_TILE], U8, align_bytes=64)
+            z_codes[i] = zc
+            z_scales[i] = zs
+            nc.vector.quantize_mx(out=zc[:].bitcast(E4M3X4), scales=zs[:], in_=z_bf[i][:])
+            written["z"] = i + 1
             passes()
 
-        build(0, 0, D_PER_TILE)
-        for kt in range(KT):
-            build(kt + 1, 0, LEAD)
-            for piece in G_BEFORE.get(kt, ()):
-                quantise_g(piece)
-            quantise(kt)
-            for piece in G_AFTER.get(kt, ()):
-                quantise_g(piece)
-            build(kt + 1, LEAD, D_PER_TILE)
+        build(0, False)
+        for i in range(TILES):
+            build(i + SCALAR_LEAD, True)
+            build(i + 1, False)
+            quantise_g(2 * i - 1)
+            quantise(i)
+            quantise_g(2 * i)

@@ -26,10 +26,10 @@ G_COLS = O // G_PIECES
 FLOPS = 2 * T * O * K
 BYTES = 4 * O * K + 2 * (T * O + B * N * D + B * V * E)
 
-STORE_GROUPS = (1, 1, 2, 4, 4, 2, 1, 1)
+STORE_GROUPS = (1,) * 16
 Z_BUFS = 6
 C_BUFS = 10
-S_BUFS = 3
+S_BUFS = 4
 SCALAR_LEAD = 3
 TAIL_V = (1, 3)
 

from contextlib import ExitStack

import concourse.mybir as mybir

BF16 = mybir.dt.bfloat16
F32 = mybir.dt.float32
U32 = mybir.dt.uint32
U8 = mybir.dt.uint8
E4M3X4 = mybir.dt.float8_e4m3fn_x4
E5M2X4 = mybir.dt.float8_e5m2_x4

P = 128
PACK = 4
B, N, V, D, E, O = 2, 32, 16, 128, 64, 512
K = D * E
T = B * N * V
N_TILE = 512
D_PER_TILE = N_TILE // E
SLAB = E * PACK
KT = K // N_TILE
OT = O // P
TILES = KT * B
G_PIECES = 2
G_COLS = O // G_PIECES

FLOPS = 2 * T * O * K
BYTES = 4 * O * K + 2 * (T * O + B * N * D + B * V * E)

STORE_GROUPS = (1,) * 16
Z_BUFS = 6
C_BUFS = 10
S_BUFS = 4
SCALAR_LEAD = 3
TAIL_V = (1, 3)


def scalar_builds(i, dd):
    return i % 2 == 1 and dd == D_PER_TILE - 1


def tile_bilinearpooling_kernel(tc, node_embed, veh_fea, W, b, grad_out, out):
    nc = tc.nc
    with ExitStack() as ctx:
        ctx.enter_context(tc.manual_schedule())
        keep = ctx.enter_context(tc.tile_pool(name="keep", bufs=1))
        zpool = ctx.enter_context(tc.tile_pool(name="zpool", bufs=Z_BUFS))
        cpool = ctx.enter_context(tc.tile_pool(name="cpool", bufs=C_BUFS))
        spool = ctx.enter_context(tc.tile_pool(name="spool", bufs=S_BUFS))
        psum = ctx.enter_context(tc.psum_pool(name="psum", bufs=8))

        g_raw = keep.tile([P, B, PACK * O], BF16)
        veh_raw = keep.tile([P, B, SLAB], BF16)
        node_raw = keep.tile([P, B, D], BF16)

        for bi in range(B):
            nc.gpsimd.dma_start(
                out=g_raw[:, bi], in_=grad_out[bi].rearrange("n (q j) o -> (n q) (j o)", j=PACK)
            )
        for q in range(PACK):
            src = veh_fea[:, PACK * q : PACK * (q + 1), :].rearrange("b j e -> b (j e)")
            nc.sync.dma_start(out=veh_raw[q:P:PACK], in_=src.unsqueeze(0).to_broadcast([N, B, SLAB]))
            nc.scalar.dma_start(out=node_raw[q:P:PACK], in_=node_embed.rearrange("b n d -> n b d"))

        node_f = keep.tile([P, B, D], F32)
        nc.scalar.copy(out=node_f[:], in_=node_raw[:])
        veh_g = keep.tile([P, B, SLAB], BF16)
        nc.vector.tensor_copy(
            out=veh_g[:].rearrange("p b (e j) -> p b e j", j=PACK),
            in_=veh_raw[:].rearrange("p b (j e) -> p b e j", j=PACK),
        )

        z_bf = {}
        z_codes = {}
        z_scales = {}

        def build(i, on_scalar):
            if not 0 <= i < TILES:
                return
            kt, bi = divmod(i, B)
            for dd in range(D_PER_TILE):
                if scalar_builds(i, dd) != on_scalar:
                    continue
                if i not in z_bf:
                    z_bf[i] = zpool.tile([P, PACK * N_TILE], BF16, name="zb", align_bytes=64)
                dcol = kt * D_PER_TILE + dd
                dst = z_bf[i][:, dd * SLAB : (dd + 1) * SLAB]
                factor = node_f[:, bi, dcol : dcol + 1]
                if on_scalar:
                    nc.scalar.activation(
                        out=dst, in_=veh_g[:, bi], func=mybir.ActivationFunctionType.Copy, scale=factor
                    )
                else:
                    nc.vector.tensor_scalar_mul(out=dst, in0=veh_g[:, bi], scalar1=factor)

        for i in range(SCALAR_LEAD):
            build(i, True)

        g_grp = keep.tile([P, B, PACK * O], BF16, align_bytes=64)
        g_codes = keep.tile([P, B, O], U32, align_bytes=64)
        g_scales = keep.tile([P, B, O], U8, align_bytes=64)
        for piece in range(B * G_PIECES):
            bi, part = divmod(piece, G_PIECES)
            nc.scalar.copy(
                out=g_grp[:, bi, part * PACK * G_COLS : (part + 1) * PACK * G_COLS].rearrange(
                    "p (o j) -> p o j", j=PACK
                ),
                in_=g_raw[:, bi].rearrange("p (j o) -> p o j", j=PACK)[
                    :, part * G_COLS : (part + 1) * G_COLS, :
                ],
            )

        group_of = {}
        first = 0
        for width in STORE_GROUPS:
            for kt in range(first, first + width):
                group_of[kt] = (first, width)
            first += width
        assert first == KT

        acc = {}
        stage = {}
        written = {"g": 0, "z": 0, "pass": 0}

        def one_pass(i, ot):
            kt, bi = divmod(i, B)
            if bi == 0:
                acc[ot] = psum.tile([P, N_TILE], F32, name="acc%d" % ot, tag="acc")
            cols = slice(ot * P, (ot + 1) * P)
            nc.tensor.matmul_mx(
                out=acc[ot][:],
                lhsT=g_codes[:, bi, cols].bitcast(E5M2X4),
                lhsT_scale=g_scales[:, bi, cols],
                rhs=z_codes[i][:].bitcast(E4M3X4),
                rhs_scale=z_scales[i][:],
                start=(bi == 0),
                stop=(bi == B - 1),
            )
            if bi < B - 1:
                return
            first_kt, width = group_of[kt]
            if kt == first_kt:
                stage[ot] = spool.tile([P, width * N_TILE], F32, name="stage%d" % ot, tag="stage%d" % ot)
            part = stage[ot][:, (kt - first_kt) * N_TILE : (kt - first_kt + 1) * N_TILE]
            if kt == KT - 1 and ot in TAIL_V:
                nc.vector.tensor_copy(out=part, in_=acc[ot][:])
            else:
                nc.scalar.copy(out=part, in_=acc[ot][:])
            if kt == first_kt + width - 1:
                nc.sync.dma_start(
                    out=out[ot * P : (ot + 1) * P, first_kt * N_TILE : (kt + 1) * N_TILE], in_=stage[ot][:]
                )

        def passes():
            while written["pass"] < TILES * OT:
                i, ot = divmod(written["pass"], OT)
                if i >= written["z"] or (i % B) * G_PIECES + ot * G_PIECES // OT >= written["g"]:
                    return
                one_pass(i, ot)
                written["pass"] += 1

        def quantise_g(piece):
            if not 0 <= piece < B * G_PIECES:
                return
            bi, part = divmod(piece, G_PIECES)
            cols = slice(part * G_COLS, (part + 1) * G_COLS)
            nc.vector.quantize_mx(
                out=g_codes[:, bi, cols].bitcast(E5M2X4),
                scales=g_scales[:, bi, cols],
                in_=g_grp[:, bi, part * PACK * G_COLS : (part + 1) * PACK * G_COLS],
            )
            written["g"] = piece + 1
            passes()

        def quantise(i):
            zc = cpool.tile([P, N_TILE], U32, align_bytes=64)
            zs = cpool.tile([P, N_TILE], U8, align_bytes=64)
            z_codes[i] = zc
            z_scales[i] = zs
            nc.vector.quantize_mx(out=zc[:].bitcast(E4M3X4), scales=zs[:], in_=z_bf[i][:])
            written["z"] = i + 1
            passes()

        build(0, False)
        for i in range(TILES):
            build(i + SCALAR_LEAD, True)
            build(i + 1, False)
            quantise_g(2 * i - 1)
            quantise(i)
            quantise_g(2 * i)
